import numpy as np
import ml_dtypes


def mxq(x, axis, fmt="e4m3"):
    dtype, down = {"e4m3": (ml_dtypes.float8_e4m3fn, 7), "e5m2": (ml_dtypes.float8_e5m2, 14)}[fmt]
    v = np.moveaxis(np.asarray(x, np.float32).astype(ml_dtypes.bfloat16).astype(np.float64), axis, -1)
    blocks = v.reshape(v.shape[:-1] + (-1, 32))
    amax = np.abs(blocks).max(-1, keepdims=True)
    byte = np.maximum(np.where(amax > 0, np.frexp(amax)[1] - 1 + 127, 0) - down, 1)
    scale = np.exp2(byte - 127.0)
    codes = (blocks / scale).astype(np.float32).astype(dtype).astype(np.float64)
    return np.moveaxis((codes * scale).reshape(v.shape), -1, axis)


WIDE = False


def mx_kscale(k):
    if not WIDE:
        return np.ones(k)
    levels = np.array([10, -10, 5, -5, 0])
    a = np.random.permutation(np.resize(levels, k // 512 * 4)).reshape(k // 512, 4)
    idx = np.arange(k)
    return np.exp2(a[idx // 512, idx % 128 // 32])


BF16 = ml_dtypes.bfloat16


def bf(x):
    return np.asarray(x, np.float32).astype(BF16)


def f64(x):
    return np.asarray(x).astype(np.float64)


E2M1 = np.array([0.0, 0.5, 1.0, 1.5, 2.0, 3.0, 4.0, 6.0, -0.0, -0.5, -1.0, -1.5, -2.0, -3.0, -4.0, -6.0])


def pack_weight(w, fmt):
    k, n = w.shape
    w = f64(bf(w)).reshape(k // 32, 32, n)
    amax = np.abs(w).max(1)
    if fmt == "e4m3":
        byte = np.frexp(amax)[1] - 1 + 127 - 7
    else:
        mant, ex = np.frexp(amax / 6.0)
        byte = np.where(mant > 0.5, ex, ex - 1) + 127
    byte = np.clip(np.where(amax > 0, byte, 1), 1, 254)
    scaled = (w * np.exp2(127.0 - byte)[:, None, :]).reshape(k, n).astype(np.float32)
    by_word = np.ascontiguousarray(scaled.reshape(k // 512, 128, 4, n).transpose(0, 1, 3, 2))
    if fmt == "e4m3":
        words = by_word.astype(ml_dtypes.float8_e4m3fn).view(np.uint8)
    else:
        c = by_word.astype(ml_dtypes.float4_e2m1fn).view(np.uint8) & 0xF
        words = c[..., 0::2] | (c[..., 1::2] << 4)
    return np.ascontiguousarray(words), np.ascontiguousarray(byte.astype(np.uint8).reshape(k // 512, 16, n))


def unpack_weight(words, scales, fmt):
    g, p, n, _ = words.shape
    if fmt == "e4m3":
        vals = np.ascontiguousarray(words).view(ml_dtypes.float8_e4m3fn).astype(np.float64)
    else:
        nib = np.empty((g, p, n, 4), np.uint8)
        nib[..., 0::2] = words & 0xF
        nib[..., 1::2] = words >> 4
        vals = E2M1[nib]
    vals = vals * np.repeat(np.exp2(scales.astype(np.float64) - 127.0), 8, axis=1)[..., None]
    return vals.transpose(0, 1, 3, 2).reshape(g * 512, n)


N, C0, H, KS, P, C, O, F, NC = 128, 1, 6, 3, 2, 512, 128, 512, 10
KK = KS * KS
OH = H - KS + 1
OP = OH // P
FC = O * OP * OP


def relu(v):
    return np.maximum(v, 0.0)


def maxpool(v):
    n, c, hh, ww = v.shape
    hp, wp = hh // P, ww // P
    return v[:, :, :hp * P, :wp * P].reshape(n, c, hp, P, wp, P).max(axis=(3, 5))


def setup_inputs():
    s = mx_kscale(C)
    t = mx_kscale(FC)
    tt = np.repeat(np.repeat(t.reshape(O, OP, OP), P, axis=1), P, axis=2)
    h = np.maximum(np.random.standard_normal((P * P, N, C, H, H)).max(0), 0.0)
    w2 = bf(np.random.standard_normal((O, C, KK, OH, OH)) * 0.8 / np.sqrt(KK * C) / s[None, :, None, None, None] * tt[:, None, None, :, :])
    b2 = bf(np.random.standard_normal((O, OH, OH)) * 0.3 * tt)
    fc1_w_words, fc1_w_scales = pack_weight(np.random.standard_normal((FC, F)) * 0.8 / np.sqrt(FC) / t[:, None], "e4m3")
    fc1_b = bf(np.random.standard_normal(F) * 0.3)
    return {
        "h_pool1": bf(h * s[None, :, None, None]),
        "w2": w2,
        "b2": b2,
        "fc1_w_words": fc1_w_words,
        "fc1_w_scales": fc1_w_scales,
        "fc1_b": fc1_b,
    }


def reference(h_pool1, w2, b2, fc1_w_words, fc1_w_scales, fc1_b):
    hq = mxq(f64(h_pool1).transpose(2, 3, 0, 1), 3, "e4m3")
    wq = mxq(f64(w2).transpose(2, 3, 4, 1, 0), 3, "e4m3")
    y = sum((hq[i:i + OH, j:j + OH] @ wq[i * KS + j]) for i in range(KS) for j in range(KS))
    y = y.transpose(2, 3, 0, 1) + f64(b2)
    g = maxpool(relu(y)).reshape(N, FC)
    return relu((mxq(g, 1, "e4m3") @ unpack_weight(fc1_w_words, fc1_w_scales, "e4m3")) + f64(fc1_b))

@@ -1,0 +1,230 @@
+import concourse.mybir as mybir
+
+F32 = mybir.dt.float32
+BF16 = mybir.dt.bfloat16
+I32 = mybir.dt.int32
+U32 = mybir.dt.uint32
+U8 = mybir.dt.uint8
+FP8X4 = mybir.dt.float8_e4m3fn_x4
+RELU = mybir.ActivationFunctionType.Relu
+
+P = 128
+PACK = 4
+N = 128
+O = 128
+KS = 3
+KK = KS * KS
+H = 6
+PIXELS = H * H
+OH = 4
+R = KK * OH * OH
+F = 512
+
+O_HALF = O // 2
+O_LOAD = 8
+N_LOAD = 32
+RUN = 4
+PIXELS_TILE = 12
+PIXELS_QUANT = 4
+
+FLOPS = 2 * N * O * 512 * R + 2 * N * 512 * F
+
+
+def tile_locallyconnectednet_pa_kernel(
+    tc, h_pool1, w2, b2, fc1_w_words, fc1_w_scales, fc1_b, out
+):
+    nc = tc.nc
+
+    def regroup(index, out_view, in_view):
+        if index % 2 == 0:
+            nc.vector.tensor_copy(out=out_view, in_=in_view)
+        else:
+            nc.scalar.copy(out=out_view, in_=in_view)
+
+    with (
+        tc.tile_pool(name="keep", bufs=1) as keep,
+        tc.tile_pool(name="raw", bufs=4) as raw_pool,
+        tc.tile_pool(name="grouped", bufs=4) as grouped_pool,
+        tc.tile_pool(name="work", bufs=2) as work,
+        tc.psum_pool(name="window", bufs=4) as window_pool,
+        tc.psum_pool(name="dense", bufs=1) as dense_pool,
+    ):
+        w_codes = keep.tile([P, R * O], U32, align_bytes=64)
+        w_scales = keep.tile([P, R * O], U8, align_bytes=64)
+        h_codes = keep.tile([P, PIXELS * N], U32, align_bytes=64)
+        h_scales = keep.tile([P, PIXELS * N], U8, align_bytes=64)
+
+        fc_codes = keep.tile([P, F], U32, align_bytes=64)
+        nc.sync.dma_start(
+            out=fc_codes[:].bitcast(I32),
+            in_=fc1_w_words.rearrange("g p n t -> (g p) (n t)").bitcast(I32),
+        )
+        fc_scales = keep.tile([P, F], U8, align_bytes=64)
+        nc.vector.memset(fc_scales[:].bitcast(I32), 0)
+        for quadrant in range(4):
+            nc.sync.dma_start(
+                out=fc_scales[32 * quadrant : 32 * quadrant + 4, :].bitcast(I32),
+                in_=fc1_w_scales[0, 4 * quadrant : 4 * quadrant + 4, :].bitcast(I32),
+            )
+        b2_bf = keep.tile([P, OH * OH], BF16)
+        nc.sync.dma_start(out=b2_bf[:], in_=b2.rearrange("o i j -> o (i j)"))
+        b2_f32 = keep.tile([P, OH * OH], F32)
+        nc.vector.tensor_copy(out=b2_f32[:], in_=b2_bf[:])
+
+        fc_b_rows = keep.tile([P, F], BF16)
+        nc.vector.memset(fc_b_rows[:], 0.0)
+        nc.sync.dma_start(out=fc_b_rows[0:1, :], in_=fc1_b.rearrange("(a f) -> a f", a=1))
+        ones = keep.tile([P, P], BF16)
+        nc.vector.memset(ones[:], 1.0)
+        fc_b_psum = dense_pool.tile([P, F], F32)
+        nc.tensor.matmul(out=fc_b_psum[:], lhsT=ones[:], rhs=fc_b_rows[:], start=True, stop=True)
+        fc_b_all = keep.tile([P, F], F32)
+        nc.scalar.copy(out=fc_b_all[:], in_=fc_b_psum[:])
+
+        def load_and_regroup_w2(half):
+            rows = []
+            for i in range(OH):
+                rows.append(
+                    grouped_pool.tile(
+                        [P, KK, OH, O_HALF * PACK], BF16, align_bytes=64, name="w_rows%d" % i,
+                        tag="grouped",
+                    )
+                )
+            for load in range(O_HALF // O_LOAD):
+                o_first = half * O_HALF + load * O_LOAD
+                raw = raw_pool.tile([P, O_LOAD * PACK, R], BF16, tag="raw")
+                nc.sync.dma_start(
+                    out=raw[:].rearrange("p (o t) r -> p o (t r)", t=PACK),
+                    in_=w2[o_first : o_first + O_LOAD].rearrange(
+                        "o (p t) k i j -> p o (t k i j)", t=PACK
+                    ),
+                )
+                by_row = raw[:].rearrange("p a (k i j) -> p i k a j", k=KK, i=OH)
+                a_first = load * O_LOAD * PACK
+                for i in range(OH):
+                    regroup(
+                        load + i,
+                        rows[i][:, :, :, a_first : a_first + O_LOAD * PACK].rearrange(
+                            "p k j a -> p k a j"
+                        ),
+                        by_row[:, i],
+                    )
+            return rows
+
+        def quantise_w2_row(half, rows, i):
+            for j in range(OH):
+                for k in range(KK):
+                    first = ((k * OH + i) * OH + j) * O + half * O_HALF
+                    nc.vector.quantize_mx(
+                        out=w_codes[:, first : first + O_HALF].bitcast(FP8X4),
+                        scales=w_scales[:, first : first + O_HALF],
+                        in_=rows[i][:, k, j, :],
+                    )
+
+        rows_a = load_and_regroup_w2(0)
+        for i in range(OH):
+            quantise_w2_row(0, rows_a, i)
+
+        h_tiles = []
+        for g in range(PIXELS // PIXELS_TILE):
+            h_tiles.append(
+                grouped_pool.tile(
+                    [P, PIXELS_TILE, N * PACK], BF16, align_bytes=64, name="h_rows%d" % g,
+                    tag="grouped",
+                )
+            )
+        for load in range(N // N_LOAD):
+            raw = raw_pool.tile([P, N_LOAD * PACK, PIXELS], BF16, tag="raw")
+            nc.sync.dma_start(
+                out=raw[:].rearrange("p (n t) x -> p n (t x)", t=PACK),
+                in_=h_pool1[load * N_LOAD : (load + 1) * N_LOAD].rearrange(
+                    "n (p t) y x -> p n (t y x)", t=PACK
+                ),
+            )
+            a_first = load * N_LOAD * PACK
+            for g in range(PIXELS // PIXELS_TILE):
+                regroup(
+                    load + g,
+                    h_tiles[g][:, :, a_first : a_first + N_LOAD * PACK].rearrange(
+                        "p (c x) a -> p c a x", x=RUN
+                    ),
+                    raw[:, :, g * PIXELS_TILE : (g + 1) * PIXELS_TILE].rearrange(
+                        "p a (c x) -> p c a x", x=RUN
+                    ),
+                )
+        for g in range(PIXELS // PIXELS_TILE):
+            for c in range(PIXELS_TILE // PIXELS_QUANT):
+                first = (g * PIXELS_TILE + c * PIXELS_QUANT) * N
+                nc.vector.quantize_mx(
+                    out=h_codes[:, first : first + PIXELS_QUANT * N].bitcast(FP8X4),
+                    scales=h_scales[:, first : first + PIXELS_QUANT * N],
+                    in_=h_tiles[g][:, c * PIXELS_QUANT : (c + 1) * PIXELS_QUANT, :].rearrange(
+                        "p x a -> p (x a)"
+                    ),
+                )
+
+        rows_b = load_and_regroup_w2(1)
+        pooled = keep.tile([P, PACK, N], F32)
+        for u in range(OH // 2):
+            windows = []
+            for v in range(OH // 2):
+                windows.append(window_pool.tile([P, 4, N], F32, name="window%d" % v, tag="window"))
+            for di in range(2):
+                i = 2 * u + di
+                quantise_w2_row(1, rows_b, i)
+                for j in range(OH):
+                    for k in range(KK):
+                        r = (k * OH + i) * OH + j
+                        x = (i + k // KS) * H + j + k % KS
+                        nc.tensor.matmul_mx(
+                            out=windows[j // 2][:, 2 * di + j % 2, :],
+                            lhsT=w_codes[:, r * O : (r + 1) * O].bitcast(FP8X4),
+                            lhsT_scale=w_scales[:, r * O : (r + 1) * O],
+                            rhs=h_codes[:, x * N : (x + 1) * N].bitcast(FP8X4),
+                            rhs_scale=h_scales[:, x * N : (x + 1) * N],
+                            start=(k == 0),
+                            stop=(k == KK - 1),
+                        )
+            for v in range(OH // 2):
+                biased = work.tile([P, 4, N], F32, tag="work")
+                for q in range(4):
+                    position = (2 * u + q // 2) * OH + 2 * v + q % 2
+                    nc.scalar.activation(
+                        out=biased[:, q, :],
+                        in_=windows[v][:, q, :],
+                        func=RELU,
+                        bias=b2_f32[:, position : position + 1],
+                        scale=1.0,
+                    )
+                nc.vector.tensor_reduce(
+                    out=pooled[:, 2 * u + v, :],
+                    in_=biased[:].rearrange("p q n -> p n q"),
+                    axis=mybir.AxisListType.X,
+                    op=mybir.AluOpType.max,
+                )
+
+        g_grouped = keep.tile([P, N, PACK], BF16, align_bytes=64)
+        nc.vector.tensor_copy(out=g_grouped[:], in_=pooled[:].rearrange("p t n -> p n t"))
+        g_codes = keep.tile([P, N], U32, align_bytes=64)
+        g_scales = keep.tile([P, N], U8, align_bytes=64)
+        nc.vector.quantize_mx(
+            out=g_codes[:].bitcast(FP8X4),
+            scales=g_scales[:],
+            in_=g_grouped[:].rearrange("p n t -> p (n t)"),
+        )
+        fc_psum = dense_pool.tile([P, F], F32)
+        nc.tensor.matmul_mx(
+            out=fc_psum[:],
+            lhsT=g_codes[:].bitcast(FP8X4),
+            lhsT_scale=g_scales[:],
+            rhs=fc_codes[:].bitcast(FP8X4),
+            rhs_scale=fc_scales[:],
+            start=True,
+            stop=True,
+        )
+        result = work.tile([P, F], F32, tag="work")
+        nc.vector.tensor_tensor(
+            out=result[:], in0=fc_psum[:], in1=fc_b_all[:], op=mybir.AluOpType.add
+        )
+        nc.vector.tensor_scalar_max(out=result[:], in0=result[:], scalar1=0.0)
+        nc.sync.dma_start(out=out[:, :], in_=result[:])

@@ -35,51 +35,32 @@ def tile_locallyconnectednet_pa_kernel(
 ):
     nc = tc.nc
 
-    def regroup(index, out_view, in_view):
-        if index % 2 == 0:
-            nc.vector.tensor_copy(out=out_view, in_=in_view)
-        else:
+    def regroup(on_scalar, out_view, in_view):
+        if on_scalar:
             nc.scalar.copy(out=out_view, in_=in_view)
+        else:
+            nc.vector.tensor_copy(out=out_view, in_=in_view)
 
     with (
         tc.tile_pool(name="keep", bufs=1) as keep,
         tc.tile_pool(name="raw", bufs=4) as raw_pool,
         tc.tile_pool(name="grouped", bufs=4) as grouped_pool,
-        tc.tile_pool(name="work", bufs=2) as work,
-        tc.psum_pool(name="window", bufs=4) as window_pool,
+        tc.tile_pool(name="work", bufs=4) as work,
+        tc.psum_pool(name="position", bufs=6) as position_pool,
         tc.psum_pool(name="dense", bufs=1) as dense_pool,
+        tc.manual_schedule(),
     ):
         w_codes = keep.tile([P, R * O], U32, align_bytes=64)
         w_scales = keep.tile([P, R * O], U8, align_bytes=64)
         h_codes = keep.tile([P, PIXELS * N], U32, align_bytes=64)
         h_scales = keep.tile([P, PIXELS * N], U8, align_bytes=64)
 
-        fc_codes = keep.tile([P, F], U32, align_bytes=64)
-        nc.sync.dma_start(
-            out=fc_codes[:].bitcast(I32),
-            in_=fc1_w_words.rearrange("g p n t -> (g p) (n t)").bitcast(I32),
-        )
         fc_scales = keep.tile([P, F], U8, align_bytes=64)
         nc.vector.memset(fc_scales[:].bitcast(I32), 0)
-        for quadrant in range(4):
-            nc.sync.dma_start(
-                out=fc_scales[32 * quadrant : 32 * quadrant + 4, :].bitcast(I32),
-                in_=fc1_w_scales[0, 4 * quadrant : 4 * quadrant + 4, :].bitcast(I32),
-            )
-        b2_bf = keep.tile([P, OH * OH], BF16)
-        nc.sync.dma_start(out=b2_bf[:], in_=b2.rearrange("o i j -> o (i j)"))
-        b2_f32 = keep.tile([P, OH * OH], F32)
-        nc.vector.tensor_copy(out=b2_f32[:], in_=b2_bf[:])
-
         fc_b_rows = keep.tile([P, F], BF16)
         nc.vector.memset(fc_b_rows[:], 0.0)
-        nc.sync.dma_start(out=fc_b_rows[0:1, :], in_=fc1_b.rearrange("(a f) -> a f", a=1))
         ones = keep.tile([P, P], BF16)
         nc.vector.memset(ones[:], 1.0)
-        fc_b_psum = dense_pool.tile([P, F], F32)
-        nc.tensor.matmul(out=fc_b_psum[:], lhsT=ones[:], rhs=fc_b_rows[:], start=True, stop=True)
-        fc_b_all = keep.tile([P, F], F32)
-        nc.scalar.copy(out=fc_b_all[:], in_=fc_b_psum[:])
 
         def load_and_regroup_w2(half):
             rows = []
@@ -103,7 +84,7 @@ def tile_locallyconnectednet_pa_kernel(
                 a_first = load * O_LOAD * PACK
                 for i in range(OH):
                     regroup(
-                        load + i,
+                        (load * OH + i) % 3 == 2,
                         rows[i][:, :, :, a_first : a_first + O_LOAD * PACK].rearrange(
                             "p k j a -> p k a j"
                         ),
@@ -125,6 +106,20 @@ def tile_locallyconnectednet_pa_kernel(
         for i in range(OH):
             quantise_w2_row(0, rows_a, i)
 
+        fc_codes = keep.tile([P, F], U32, align_bytes=64)
+        nc.sync.dma_start(
+            out=fc_codes[:].bitcast(I32),
+            in_=fc1_w_words.rearrange("g p n t -> (g p) (n t)").bitcast(I32),
+        )
+        for quadrant in range(4):
+            nc.sync.dma_start(
+                out=fc_scales[32 * quadrant : 32 * quadrant + 4, :].bitcast(I32),
+                in_=fc1_w_scales[0, 4 * quadrant : 4 * quadrant + 4, :].bitcast(I32),
+            )
+        b2_bf = keep.tile([P, OH * OH], BF16)
+        nc.sync.dma_start(out=b2_bf[:], in_=b2.rearrange("o i j -> o (i j)"))
+        nc.sync.dma_start(out=fc_b_rows[0:1, :], in_=fc1_b.rearrange("(a f) -> a f", a=1))
+
         h_tiles = []
         for g in range(PIXELS // PIXELS_TILE):
             h_tiles.append(
@@ -144,7 +139,7 @@ def tile_locallyconnectednet_pa_kernel(
             a_first = load * N_LOAD * PACK
             for g in range(PIXELS // PIXELS_TILE):
                 regroup(
-                    load + g,
+                    g > 0,
                     h_tiles[g][:, :, a_first : a_first + N_LOAD * PACK].rearrange(
                         "p (c x) a -> p c a x", x=RUN
                     ),
@@ -163,48 +158,62 @@ def tile_locallyconnectednet_pa_kernel(
                     ),
                 )
 
+        b2_f32 = keep.tile([P, OH * OH], F32)
+        nc.vector.tensor_copy(out=b2_f32[:], in_=b2_bf[:])
+        fc_b_psum = dense_pool.tile([P, F], F32)
+        nc.tensor.matmul(out=fc_b_psum[:], lhsT=ones[:], rhs=fc_b_rows[:], start=True, stop=True)
+        fc_b_all = keep.tile([P, F], F32)
+        nc.scalar.copy(out=fc_b_all[:], in_=fc_b_psum[:])
+
         rows_b = load_and_regroup_w2(1)
-        pooled = keep.tile([P, PACK, N], F32)
-        for u in range(OH // 2):
-            windows = []
-            for v in range(OH // 2):
-                windows.append(window_pool.tile([P, 4, N], F32, name="window%d" % v, tag="window"))
-            for di in range(2):
-                i = 2 * u + di
-                quantise_w2_row(1, rows_b, i)
-                for j in range(OH):
-                    for k in range(KK):
-                        r = (k * OH + i) * OH + j
-                        x = (i + k // KS) * H + j + k % KS
-                        nc.tensor.matmul_mx(
-                            out=windows[j // 2][:, 2 * di + j % 2, :],
-                            lhsT=w_codes[:, r * O : (r + 1) * O].bitcast(FP8X4),
-                            lhsT_scale=w_scales[:, r * O : (r + 1) * O],
-                            rhs=h_codes[:, x * N : (x + 1) * N].bitcast(FP8X4),
-                            rhs_scale=h_scales[:, x * N : (x + 1) * N],
-                            start=(k == 0),
-                            stop=(k == KK - 1),
-                        )
-            for v in range(OH // 2):
-                biased = work.tile([P, 4, N], F32, tag="work")
-                for q in range(4):
-                    position = (2 * u + q // 2) * OH + 2 * v + q % 2
-                    nc.scalar.activation(
-                        out=biased[:, q, :],
-                        in_=windows[v][:, q, :],
-                        func=RELU,
-                        bias=b2_f32[:, position : position + 1],
-                        scale=1.0,
+        g_grouped = keep.tile([P, N, PACK], BF16, align_bytes=64)
+
+        def convolve_row(i, biased):
+            for j in range(OH):
+                acc = position_pool.tile([P, N], F32, tag="acc")
+                for k in range(KK):
+                    r = (k * OH + i) * OH + j
+                    x = (i + k // KS) * H + j + k % KS
+                    nc.tensor.matmul_mx(
+                        out=acc[:],
+                        lhsT=w_codes[:, r * O : (r + 1) * O].bitcast(FP8X4),
+                        lhsT_scale=w_scales[:, r * O : (r + 1) * O],
+                        rhs=h_codes[:, x * N : (x + 1) * N].bitcast(FP8X4),
+                        rhs_scale=h_scales[:, x * N : (x + 1) * N],
+                        start=(k == 0),
+                        stop=(k == KK - 1),
                     )
-                nc.vector.tensor_reduce(
-                    out=pooled[:, 2 * u + v, :],
-                    in_=biased[:].rearrange("p q n -> p n q"),
-                    axis=mybir.AxisListType.X,
-                    op=mybir.AluOpType.max,
+                nc.scalar.activation(
+                    out=biased[j // 2][:, 2 * (i % 2) + j % 2, :],
+                    in_=acc[:],
+                    func=RELU,
+                    bias=b2_f32[:, i * OH + j : i * OH + j + 1],
+                    scale=1.0,
                 )
 
-        g_grouped = keep.tile([P, N, PACK], BF16, align_bytes=64)
-        nc.vector.tensor_copy(out=g_grouped[:], in_=pooled[:].rearrange("p t n -> p n t"))
+        def pool_windows(u, biased):
+            for v in range(OH // 2):
+                with nc.allow_low_precision(reason="a maximum is exact; this is g's one rounding"):
+                    nc.vector.tensor_reduce(
+                        out=g_grouped[:, :, 2 * u + v],
+                        in_=biased[v][:].rearrange("p q n -> p n q"),
+                        axis=mybir.AxisListType.X,
+                        op=mybir.AluOpType.max,
+                    )
+
+        biased_of = {}
+        for i in range(OH):
+            quantise_w2_row(1, rows_b, i)
+            if i % 2 == 0:
+                if i > 0:
+                    pool_windows(i // 2 - 1, biased_of[i // 2 - 1])
+                biased_of[i // 2] = [
+                    work.tile([P, 4, N], F32, name="biased%d" % v, tag="work")
+                    for v in range(OH // 2)
+                ]
+            convolve_row(i, biased_of[i // 2])
+        pool_windows(OH // 2 - 1, biased_of[OH // 2 - 1])
+
         g_codes = keep.tile([P, N], U32, align_bytes=64)
         g_scales = keep.tile([P, N], U8, align_bytes=64)
         nc.vector.quantize_mx(

@@ -1,4 +1,5 @@
 import concourse.mybir as mybir
+from concourse.masks import make_identity
 
 F32 = mybir.dt.float32
 BF16 = mybir.dt.bfloat16
@@ -12,20 +13,26 @@ P = 128
 PACK = 4
 N = 128
 O = 128
+C = 512
 KS = 3
 KK = KS * KS
 H = 6
 PIXELS = H * H
+PAIRS = PIXELS // 2
 OH = 4
 R = KK * OH * OH
 F = 512
 
 O_HALF = O // 2
 O_LOAD = 8
-N_LOAD = 32
-RUN = 4
-PIXELS_TILE = 12
-PIXELS_QUANT = 4
+LOADS = O // O_LOAD
+LOADS_HALF = O_HALF // O_LOAD
+H_LOADS = 4
+PIXELS_QUANT = 2
+H_SLOTS = 4
+BANKS = 7
+RAW_BUFS = 4
+FLEX_LOAD = 12
 
 FLOPS = 2 * N * O * 512 * R + 2 * N * 512 * F
 
@@ -35,7 +42,7 @@ def tile_locallyconnectednet_pa_kernel(
 ):
     nc = tc.nc
 
-    def regroup(on_scalar, out_view, in_view):
+    def copy(on_scalar, out_view, in_view):
         if on_scalar:
             nc.scalar.copy(out=out_view, in_=in_view)
         else:
@@ -43,70 +50,168 @@ def tile_locallyconnectednet_pa_kernel(
 
     with (
         tc.tile_pool(name="keep", bufs=1) as keep,
-        tc.tile_pool(name="raw", bufs=4) as raw_pool,
-        tc.tile_pool(name="grouped", bufs=4) as grouped_pool,
-        tc.tile_pool(name="work", bufs=4) as work,
-        tc.psum_pool(name="position", bufs=6) as position_pool,
+        tc.tile_pool(name="big", bufs=1) as big,
+        tc.tile_pool(name="raw", bufs=RAW_BUFS) as raw_pool,
+        tc.tile_pool(name="flex", bufs=1) as flex,
+        tc.tile_pool(name="grouped", bufs=OH) as grouped_pool,
+        tc.psum_pool(name="bank", bufs=BANKS) as bank_pool,
         tc.psum_pool(name="dense", bufs=1) as dense_pool,
         tc.manual_schedule(),
     ):
-        w_codes = keep.tile([P, R * O], U32, align_bytes=64)
         w_scales = keep.tile([P, R * O], U8, align_bytes=64)
         h_codes = keep.tile([P, PIXELS * N], U32, align_bytes=64)
         h_scales = keep.tile([P, PIXELS * N], U8, align_bytes=64)
-
+        fc_codes = keep.tile([P, F], U32, align_bytes=64)
         fc_scales = keep.tile([P, F], U8, align_bytes=64)
+        fc_b_all = keep.tile([P, F], BF16)
+        b2_bf = keep.tile([P, OH * OH], BF16)
+        b2_f32 = keep.tile([P, OH * OH], F32)
+        ident = keep.tile([P, P], F32)
+        make_identity(nc, ident[:])
         nc.vector.memset(fc_scales[:].bitcast(I32), 0)
-        fc_b_rows = keep.tile([P, F], BF16)
-        nc.vector.memset(fc_b_rows[:], 0.0)
-        ones = keep.tile([P, P], BF16)
-        nc.vector.memset(ones[:], 1.0)
 
-        def load_and_regroup_w2(half):
-            rows = []
-            for i in range(OH):
-                rows.append(
-                    grouped_pool.tile(
-                        [P, KK, OH, O_HALF * PACK], BF16, align_bytes=64, name="w_rows%d" % i,
-                        tag="grouped",
-                    )
-                )
-            for load in range(O_HALF // O_LOAD):
-                o_first = half * O_HALF + load * O_LOAD
+        nc.sync.dma_start(out=b2_bf[:], in_=b2.rearrange("o i j -> o (i j)"))
+        h_raw = big.tile([P, C * PIXELS], BF16, align_bytes=64, tag="big")
+        h_flat = h_pool1.rearrange("n c y x -> n (c y x)")
+        h_step = C * PIXELS // H_LOADS
+        for load in range(H_LOADS):
+            nc.sync.dma_start(
+                out=h_raw[:, load * h_step : (load + 1) * h_step],
+                in_=h_flat[:, load * h_step : (load + 1) * h_step],
+            )
+        nc.vector.tensor_copy(out=b2_f32[:], in_=b2_bf[:])
+
+        raws = {}
+
+        def load_w2(s):
+            if s == FLEX_LOAD:
+                raw = flex.tile([P, O_LOAD * PACK, R], BF16, align_bytes=64, tag="flex")
+            else:
                 raw = raw_pool.tile([P, O_LOAD * PACK, R], BF16, tag="raw")
-                nc.sync.dma_start(
-                    out=raw[:].rearrange("p (o t) r -> p o (t r)", t=PACK),
-                    in_=w2[o_first : o_first + O_LOAD].rearrange(
-                        "o (p t) k i j -> p o (t k i j)", t=PACK
-                    ),
-                )
-                by_row = raw[:].rearrange("p a (k i j) -> p i k a j", k=KK, i=OH)
-                a_first = load * O_LOAD * PACK
-                for i in range(OH):
-                    regroup(
-                        (load * OH + i) % 3 == 2,
-                        rows[i][:, :, :, a_first : a_first + O_LOAD * PACK].rearrange(
-                            "p k j a -> p k a j"
-                        ),
-                        by_row[:, i],
-                    )
-            return rows
+            nc.sync.dma_start(
+                out=raw[:].rearrange("p (o t) r -> p o (t r)", t=PACK),
+                in_=w2[s * O_LOAD : (s + 1) * O_LOAD].rearrange(
+                    "o (p t) k i j -> p o (t k i j)", t=PACK
+                ),
+            )
+            raws[s] = raw
 
-        def quantise_w2_row(half, rows, i):
+        def new_row(i):
+            row = grouped_pool.tile(
+                [P, KK, OH, O_HALF * PACK], BF16, align_bytes=64, name="w_row%d" % i, tag="grouped"
+            )
+            return row
+
+        rows = [[new_row(i) for i in range(OH)], [None] * OH]
+
+        def regroup(s, i, on_scalar):
+            half, load = divmod(s, LOADS_HALF)
+            a_first = load * O_LOAD * PACK
+            copy(
+                on_scalar,
+                rows[half][i][:, :, :, a_first : a_first + O_LOAD * PACK].rearrange(
+                    "p k j a -> p k a j"
+                ),
+                raws[s][:].rearrange("p a (k i j) -> p i k a j", k=KK, i=OH)[:, i],
+            )
+
+        for s in range(RAW_BUFS):
+            load_w2(s)
+
+        words = h_raw[:].bitcast(F32).rearrange("n (p t s) -> n t s p", t=PACK, s=PAIRS)
+        h_grouped = flex.tile([P, H_SLOTS, PIXELS_QUANT, N * PACK], BF16, align_bytes=64, tag="flex")
+        banks = {}
+
+        def transpose_pair(s):
+            xt = bank_pool.tile([P, PACK, N], F32, tag="bank")
+            for t in range(PACK):
+                nc.tensor.transpose(xt[:, t, :], words[:, t, s, :], ident[:])
+            banks[s] = xt
+
+        def copy_out(s, on_scalar):
+            copy(
+                on_scalar,
+                h_grouped[:, s % H_SLOTS].rearrange("p e (n t) -> p e n t", t=PACK),
+                banks[s][:]
+                .rearrange("p t n -> p (t n)")
+                .bitcast(BF16)
+                .rearrange("p (t n e) -> p e n t", t=PACK, e=2),
+            )
+
+        def quantise_h(m):
+            first = m * PIXELS_QUANT * N
+            nc.vector.quantize_mx(
+                out=h_codes[:, first : first + PIXELS_QUANT * N].bitcast(FP8X4),
+                scales=h_scales[:, first : first + PIXELS_QUANT * N],
+                in_=h_grouped[:, m % H_SLOTS].rearrange("p x a -> p (x a)"),
+            )
+
+        for s in range(BANKS):
+            transpose_pair(s)
+        for s in range(4):
+            copy_out(s, s % 2 == 0)
+            transpose_pair(BANKS + s)
+        for s in range(4):
+            quantise_h(s)
+
+        for s in range(4, PAIRS + 2):
+            if s < PAIRS:
+                copy_out(s, True)
+                if BANKS + s < PAIRS:
+                    transpose_pair(BANKS + s)
+            load, i = divmod(s - 4, OH)
+            regroup(load, i, False)
+            if s < PAIRS:
+                quantise_h(s)
+            if i == OH - 1:
+                load_w2(load + RAW_BUFS)
+        for s in range(4, LOADS_HALF):
+            regroup(s, 0, False)
+            regroup(s, 1, False)
+            regroup(s, 2, True)
+            regroup(s, 3, True)
+            load_w2(s + RAW_BUFS)
+        load_w2(FLEX_LOAD)
+
+        w_codes = big.tile([P, R * O], U32, align_bytes=64, tag="big")
+
+        def quantise_w2_row(half, i):
             for j in range(OH):
                 for k in range(KK):
                     first = ((k * OH + i) * OH + j) * O + half * O_HALF
                     nc.vector.quantize_mx(
                         out=w_codes[:, first : first + O_HALF].bitcast(FP8X4),
                         scales=w_scales[:, first : first + O_HALF],
-                        in_=rows[i][:, k, j, :],
+                        in_=rows[half][i][:, k, j, :],
                     )
 
-        rows_a = load_and_regroup_w2(0)
-        for i in range(OH):
-            quantise_w2_row(0, rows_a, i)
+        first_b = LOADS_HALF
+        quantise_w2_row(0, 0)
+        rows[1][0] = new_row(0)
+        regroup(first_b, 0, True)
+        quantise_w2_row(0, 1)
+        rows[1][1] = new_row(1)
+        regroup(first_b, 1, True)
+        regroup(first_b + 1, 0, True)
+        quantise_w2_row(0, 2)
+        rows[1][2] = new_row(2)
+        regroup(first_b, 2, True)
+        regroup(first_b + 1, 1, True)
+        regroup(first_b + 1, 2, True)
+        quantise_w2_row(0, 3)
+        rows[1][3] = new_row(3)
+        regroup(first_b, 3, False)
+        load_w2(13)
+        regroup(first_b + 1, 3, False)
+        load_w2(14)
+        for s in range(first_b + 2, LOADS):
+            regroup(s, 0, False)
+            regroup(s, 1, False)
+            regroup(s, 2, True)
+            regroup(s, 3, True)
+            if s == first_b + 2:
+                load_w2(15)
 
-        fc_codes = keep.tile([P, F], U32, align_bytes=64)
         nc.sync.dma_start(
             out=fc_codes[:].bitcast(I32),
             in_=fc1_w_words.rearrange("g p n t -> (g p) (n t)").bitcast(I32),
@@ -116,61 +221,14 @@ def tile_locallyconnectednet_pa_kernel(
                 out=fc_scales[32 * quadrant : 32 * quadrant + 4, :].bitcast(I32),
                 in_=fc1_w_scales[0, 4 * quadrant : 4 * quadrant + 4, :].bitcast(I32),
             )
-        b2_bf = keep.tile([P, OH * OH], BF16)
-        nc.sync.dma_start(out=b2_bf[:], in_=b2.rearrange("o i j -> o (i j)"))
-        nc.sync.dma_start(out=fc_b_rows[0:1, :], in_=fc1_b.rearrange("(a f) -> a f", a=1))
+        nc.sync.dma_start(out=fc_b_all[:], in_=fc1_b.partition_broadcast(P))
 
-        h_tiles = []
-        for g in range(PIXELS // PIXELS_TILE):
-            h_tiles.append(
-                grouped_pool.tile(
-                    [P, PIXELS_TILE, N * PACK], BF16, align_bytes=64, name="h_rows%d" % g,
-                    tag="grouped",
-                )
-            )
-        for load in range(N // N_LOAD):
-            raw = raw_pool.tile([P, N_LOAD * PACK, PIXELS], BF16, tag="raw")
-            nc.sync.dma_start(
-                out=raw[:].rearrange("p (n t) x -> p n (t x)", t=PACK),
-                in_=h_pool1[load * N_LOAD : (load + 1) * N_LOAD].rearrange(
-                    "n (p t) y x -> p n (t y x)", t=PACK
-                ),
-            )
-            a_first = load * N_LOAD * PACK
-            for g in range(PIXELS // PIXELS_TILE):
-                regroup(
-                    g > 0,
-                    h_tiles[g][:, :, a_first : a_first + N_LOAD * PACK].rearrange(
-                        "p (c x) a -> p c a x", x=RUN
-                    ),
-                    raw[:, :, g * PIXELS_TILE : (g + 1) * PIXELS_TILE].rearrange(
-                        "p a (c x) -> p c a x", x=RUN
-                    ),
-                )
-        for g in range(PIXELS // PIXELS_TILE):
-            for c in range(PIXELS_TILE // PIXELS_QUANT):
-                first = (g * PIXELS_TILE + c * PIXELS_QUANT) * N
-                nc.vector.quantize_mx(
-                    out=h_codes[:, first : first + PIXELS_QUANT * N].bitcast(FP8X4),
-                    scales=h_scales[:, first : first + PIXELS_QUANT * N],
-                    in_=h_tiles[g][:, c * PIXELS_QUANT : (c + 1) * PIXELS_QUANT, :].rearrange(
-                        "p x a -> p (x a)"
-                    ),
-                )
-
-        b2_f32 = keep.tile([P, OH * OH], F32)
-        nc.vector.tensor_copy(out=b2_f32[:], in_=b2_bf[:])
-        fc_b_psum = dense_pool.tile([P, F], F32)
-        nc.tensor.matmul(out=fc_b_psum[:], lhsT=ones[:], rhs=fc_b_rows[:], start=True, stop=True)
-        fc_b_all = keep.tile([P, F], F32)
-        nc.scalar.copy(out=fc_b_all[:], in_=fc_b_psum[:])
-
-        rows_b = load_and_regroup_w2(1)
         g_grouped = keep.tile([P, N, PACK], BF16, align_bytes=64)
+        biased_all = flex.tile([P, OH, 4, N], F32, align_bytes=64, tag="flex")
 
-        def convolve_row(i, biased):
+        def convolve_row(i):
             for j in range(OH):
-                acc = position_pool.tile([P, N], F32, tag="acc")
+                acc = bank_pool.tile([P, N], F32, tag="bank")
                 for k in range(KK):
                     r = (k * OH + i) * OH + j
                     x = (i + k // KS) * H + j + k % KS
@@ -184,35 +242,29 @@ def tile_locallyconnectednet_pa_kernel(
                         stop=(k == KK - 1),
                     )
                 nc.scalar.activation(
-                    out=biased[j // 2][:, 2 * (i % 2) + j % 2, :],
+                    out=biased_all[:, 2 * (i // 2) + j // 2, 2 * (i % 2) + j % 2, :],
                     in_=acc[:],
                     func=RELU,
                     bias=b2_f32[:, i * OH + j : i * OH + j + 1],
                     scale=1.0,
                 )
 
-        def pool_windows(u, biased):
+        def pool_windows(u):
             for v in range(OH // 2):
                 with nc.allow_low_precision(reason="a maximum is exact; this is g's one rounding"):
                     nc.vector.tensor_reduce(
                         out=g_grouped[:, :, 2 * u + v],
-                        in_=biased[v][:].rearrange("p q n -> p n q"),
+                        in_=biased_all[:, 2 * u + v].rearrange("p q n -> p n q"),
                         axis=mybir.AxisListType.X,
                         op=mybir.AluOpType.max,
                     )
 
-        biased_of = {}
         for i in range(OH):
-            quantise_w2_row(1, rows_b, i)
-            if i % 2 == 0:
-                if i > 0:
-                    pool_windows(i // 2 - 1, biased_of[i // 2 - 1])
-                biased_of[i // 2] = [
-                    work.tile([P, 4, N], F32, name="biased%d" % v, tag="work")
-                    for v in range(OH // 2)
-                ]
-            convolve_row(i, biased_of[i // 2])
-        pool_windows(OH // 2 - 1, biased_of[OH // 2 - 1])
+            quantise_w2_row(1, i)
+            if i == 2:
+                pool_windows(0)
+            convolve_row(i)
+        pool_windows(1)
 
         g_codes = keep.tile([P, N], U32, align_bytes=64)
         g_scales = keep.tile([P, N], U8, align_bytes=64)
@@ -231,7 +283,7 @@ def tile_locallyconnectednet_pa_kernel(
             start=True,
             stop=True,
         )
-        result = work.tile([P, F], F32, tag="work")
+        result = raw_pool.tile([P, F], F32, tag="raw")
         nc.vector.tensor_tensor(
             out=result[:], in0=fc_psum[:], in1=fc_b_all[:], op=mybir.AluOpType.add
         )

@@ -31,8 +31,8 @@ H_LOADS = 4
 PIXELS_QUANT = 2
 H_SLOTS = 4
 BANKS = 7
-RAW_BUFS = 4
-FLEX_LOAD = 12
+RAW_BUFS = 5
+FLEX_LOAD = 13
 
 FLOPS = 2 * N * O * 512 * R + 2 * N * 512 * F
 
@@ -61,13 +61,11 @@ def tile_locallyconnectednet_pa_kernel(
         w_scales = keep.tile([P, R * O], U8, align_bytes=64)
         h_codes = keep.tile([P, PIXELS * N], U32, align_bytes=64)
         h_scales = keep.tile([P, PIXELS * N], U8, align_bytes=64)
-        fc_codes = keep.tile([P, F], U32, align_bytes=64)
-        fc_scales = keep.tile([P, F], U8, align_bytes=64)
-        fc_b_all = keep.tile([P, F], BF16)
         b2_bf = keep.tile([P, OH * OH], BF16)
         b2_f32 = keep.tile([P, OH * OH], F32)
         ident = keep.tile([P, P], F32)
         make_identity(nc, ident[:])
+        fc_scales = keep.tile([P, F], U8, align_bytes=64)
         nc.vector.memset(fc_scales[:].bitcast(I32), 0)
 
         nc.sync.dma_start(out=b2_bf[:], in_=b2.rearrange("o i j -> o (i j)"))
@@ -87,7 +85,7 @@ def tile_locallyconnectednet_pa_kernel(
             if s == FLEX_LOAD:
                 raw = flex.tile([P, O_LOAD * PACK, R], BF16, align_bytes=64, tag="flex")
             else:
-                raw = raw_pool.tile([P, O_LOAD * PACK, R], BF16, tag="raw")
+                raw = raw_pool.tile([P, O_LOAD * PACK, R], BF16, align_bytes=64, tag="raw")
             nc.sync.dma_start(
                 out=raw[:].rearrange("p (o t) r -> p o (t r)", t=PACK),
                 in_=w2[s * O_LOAD : (s + 1) * O_LOAD].rearrange(
@@ -117,6 +115,14 @@ def tile_locallyconnectednet_pa_kernel(
 
         for s in range(RAW_BUFS):
             load_w2(s)
+
+        def vector_rows(s):
+            left = LOADS_HALF - 1 - s % LOADS_HALF
+            if left == 0:
+                return 1
+            if left <= 2 and s >= LOADS_HALF:
+                return 3
+            return 2
 
         words = h_raw[:].bitcast(F32).rearrange("n (p t s) -> n t s p", t=PACK, s=PAIRS)
         h_grouped = flex.tile([P, H_SLOTS, PIXELS_QUANT, N * PACK], BF16, align_bytes=64, tag="flex")
@@ -166,10 +172,8 @@ def tile_locallyconnectednet_pa_kernel(
             if i == OH - 1:
                 load_w2(load + RAW_BUFS)
         for s in range(4, LOADS_HALF):
-            regroup(s, 0, False)
-            regroup(s, 1, False)
-            regroup(s, 2, True)
-            regroup(s, 3, True)
+            for i in range(OH):
+                regroup(s, i, i >= vector_rows(s))
             load_w2(s + RAW_BUFS)
         load_w2(FLEX_LOAD)
 
@@ -201,19 +205,18 @@ def tile_locallyconnectednet_pa_kernel(
         quantise_w2_row(0, 3)
         rows[1][3] = new_row(3)
         regroup(first_b, 3, False)
-        load_w2(13)
-        regroup(first_b + 1, 3, False)
         load_w2(14)
-        for s in range(first_b + 2, LOADS):
-            regroup(s, 0, False)
-            regroup(s, 1, False)
-            regroup(s, 2, True)
-            regroup(s, 3, True)
-            if s == first_b + 2:
-                load_w2(15)
+        regroup(first_b + 1, 3, False)
+        load_w2(15)
+        for i in range(OH):
+            regroup(first_b + 2, i, i >= vector_rows(first_b + 2))
 
+        tail_words = raw_pool.tile([P, O_LOAD * PACK * R // 2], U32, align_bytes=64, tag="raw")
+        fc_codes = tail_words[:, 0:F]
+        g_codes = tail_words[:, F : F + N]
+        g_scales = tail_words[:, 640:672].bitcast(U8)
         nc.sync.dma_start(
-            out=fc_codes[:].bitcast(I32),
+            out=fc_codes.bitcast(I32),
             in_=fc1_w_words.rearrange("g p n t -> (g p) (n t)").bitcast(I32),
         )
         for quadrant in range(4):
@@ -221,9 +224,16 @@ def tile_locallyconnectednet_pa_kernel(
                 out=fc_scales[32 * quadrant : 32 * quadrant + 4, :].bitcast(I32),
                 in_=fc1_w_scales[0, 4 * quadrant : 4 * quadrant + 4, :].bitcast(I32),
             )
-        nc.sync.dma_start(out=fc_b_all[:], in_=fc1_b.partition_broadcast(P))
+        for i in range(OH):
+            regroup(first_b + 3, i, i >= vector_rows(first_b + 3))
+        tail_values = raw_pool.tile([P, 2, F], BF16, align_bytes=64, tag="raw")
+        fc_b_all = tail_values[:, 0, :]
+        g_grouped = tail_values[:, 1, :].rearrange("p (n t) -> p n t", t=PACK)
+        nc.sync.dma_start(out=fc_b_all, in_=fc1_b.partition_broadcast(P))
+        for s in range(first_b + 4, LOADS):
+            for i in range(OH):
+                regroup(s, i, i >= vector_rows(s))
 
-        g_grouped = keep.tile([P, N, PACK], BF16, align_bytes=64)
         biased_all = flex.tile([P, OH, 4, N], F32, align_bytes=64, tag="flex")
 
         def convolve_row(i):
@@ -266,26 +276,24 @@ def tile_locallyconnectednet_pa_kernel(
             convolve_row(i)
         pool_windows(1)
 
-        g_codes = keep.tile([P, N], U32, align_bytes=64)
-        g_scales = keep.tile([P, N], U8, align_bytes=64)
         nc.vector.quantize_mx(
-            out=g_codes[:].bitcast(FP8X4),
-            scales=g_scales[:],
-            in_=g_grouped[:].rearrange("p n t -> p (n t)"),
+            out=g_codes.bitcast(FP8X4),
+            scales=g_scales,
+            in_=g_grouped.rearrange("p n t -> p (n t)"),
         )
         fc_psum = dense_pool.tile([P, F], F32)
         nc.tensor.matmul_mx(
             out=fc_psum[:],
-            lhsT=g_codes[:].bitcast(FP8X4),
-            lhsT_scale=g_scales[:],
-            rhs=fc_codes[:].bitcast(FP8X4),
+            lhsT=g_codes.bitcast(FP8X4),
+            lhsT_scale=g_scales,
+            rhs=fc_codes.bitcast(FP8X4),
             rhs_scale=fc_scales[:],
             start=True,
             stop=True,
         )
-        result = raw_pool.tile([P, F], F32, tag="raw")
+        result = raw_pool.tile([P, F], F32, align_bytes=64, tag="raw")
         nc.vector.tensor_tensor(
-            out=result[:], in0=fc_psum[:], in1=fc_b_all[:], op=mybir.AluOpType.add
+            out=result[:], in0=fc_psum[:], in1=fc_b_all, op=mybir.AluOpType.add
         )
         nc.vector.tensor_scalar_max(out=result[:], in0=result[:], scalar1=0.0)
         nc.sync.dma_start(out=out[:, :], in_=result[:])

@@ -120,7 +120,7 @@ def tile_locallyconnectednet_pa_kernel(
             left = LOADS_HALF - 1 - s % LOADS_HALF
             if left == 0:
                 return 1
-            if left <= 2 and s >= LOADS_HALF:
+            if s == LOADS - 3:
                 return 3
             return 2
 
@@ -157,8 +157,9 @@ def tile_locallyconnectednet_pa_kernel(
         for s in range(4):
             copy_out(s, s % 2 == 0)
             transpose_pair(BANKS + s)
-        for s in range(4):
-            quantise_h(s)
+            if s % 2 == 1:
+                quantise_h(s - 1)
+                quantise_h(s)
 
         for s in range(4, PAIRS + 2):
             if s < PAIRS:
@@ -230,9 +231,13 @@ def tile_locallyconnectednet_pa_kernel(
         fc_b_all = tail_values[:, 0, :]
         g_grouped = tail_values[:, 1, :].rearrange("p (n t) -> p n t", t=PACK)
         nc.sync.dma_start(out=fc_b_all, in_=fc1_b.partition_broadcast(P))
+        late = []
         for s in range(first_b + 4, LOADS):
             for i in range(OH):
-                regroup(s, i, i >= vector_rows(s))
+                if i == OH - 1 and s >= LOADS - 2:
+                    late.append(s)
+                else:
+                    regroup(s, i, i >= vector_rows(s))
 
         biased_all = flex.tile([P, OH, 4, N], F32, align_bytes=64, tag="flex")
 
@@ -271,9 +276,11 @@ def tile_locallyconnectednet_pa_kernel(
 
         for i in range(OH):
             quantise_w2_row(1, i)
-            if i == 2:
-                pool_windows(0)
             convolve_row(i)
+            if i == 0:
+                for s in late:
+                    regroup(s, OH - 1, True)
+        pool_windows(0)
         pool_windows(1)
 
         nc.vector.quantize_mx(

@@ -108,9 +108,9 @@ def tile_locallyconnectednet_pa_kernel(
             copy(
                 on_scalar,
                 rows[half][i][:, :, :, a_first : a_first + O_LOAD * PACK].rearrange(
-                    "p k j a -> p k a j"
+                    "p k j (h a) -> p h k a j", h=2
                 ),
-                raws[s][:].rearrange("p a (k i j) -> p i k a j", k=KK, i=OH)[:, i],
+                raws[s][:].rearrange("p (h a) (k i j) -> p i h k a j", h=2, k=KK, i=OH)[:, i],
             )
 
         for s in range(RAW_BUFS):

@@ -86,12 +86,17 @@ def tile_locallyconnectednet_pa_kernel(
                 raw = flex.tile([P, O_LOAD * PACK, R], BF16, align_bytes=64, tag="flex")
             else:
                 raw = raw_pool.tile([P, O_LOAD * PACK, R], BF16, align_bytes=64, tag="raw")
-            nc.sync.dma_start(
-                out=raw[:].rearrange("p (o t) r -> p o (t r)", t=PACK),
-                in_=w2[s * O_LOAD : (s + 1) * O_LOAD].rearrange(
-                    "o (p t) k i j -> p o (t k i j)", t=PACK
-                ),
-            )
+            parts = 2 if s == LOADS - 1 else 1
+            o_part = O_LOAD // parts
+            for part in range(parts):
+                nc.sync.dma_start(
+                    out=raw[:, part * o_part * PACK : (part + 1) * o_part * PACK, :].rearrange(
+                        "p (o t) r -> p o (t r)", t=PACK
+                    ),
+                    in_=w2[s * O_LOAD + part * o_part : s * O_LOAD + (part + 1) * o_part].rearrange(
+                        "o (p t) k i j -> p o (t k i j)", t=PACK
+                    ),
+                )
             raws[s] = raw
 
         def new_row(i):
@@ -102,15 +107,17 @@ def tile_locallyconnectednet_pa_kernel(
 
         rows = [[new_row(i) for i in range(OH)], [None] * OH]
 
-        def regroup(s, i, on_scalar):
+        def regroup(s, i, on_scalar, first=0, count=O_LOAD * PACK):
             half, load = divmod(s, LOADS_HALF)
-            a_first = load * O_LOAD * PACK
+            a_first = load * O_LOAD * PACK + first
             copy(
                 on_scalar,
-                rows[half][i][:, :, :, a_first : a_first + O_LOAD * PACK].rearrange(
+                rows[half][i][:, :, :, a_first : a_first + count].rearrange(
                     "p k j (h a) -> p h k a j", h=2
                 ),
-                raws[s][:].rearrange("p (h a) (k i j) -> p i h k a j", h=2, k=KK, i=OH)[:, i],
+                raws[s][:, first : first + count, :].rearrange(
+                    "p (h a) (k i j) -> p i h k a j", h=2, k=KK, i=OH
+                )[:, i],
             )
 
         for s in range(RAW_BUFS):
@@ -236,10 +243,14 @@ def tile_locallyconnectednet_pa_kernel(
             for i in range(OH):
                 if i == OH - 1 and s >= LOADS - 2:
                     late.append(s)
+                elif i == 0 and s == LOADS - 1:
+                    for part in range(2):
+                        regroup(s, i, False, part * O_LOAD * PACK // 2, O_LOAD * PACK // 2)
                 else:
                     regroup(s, i, i >= vector_rows(s))
 
-        biased_all = flex.tile([P, OH, 4, N], F32, align_bytes=64, tag="flex")
+        biased_all = flex.tile([P, 4, N, PACK], BF16, align_bytes=64, tag="flex")
+        tops = raw_pool.tile([P, 2, N * PACK], BF16, align_bytes=64, tag="raw")
 
         def convolve_row(i):
             for j in range(OH):
@@ -257,22 +268,16 @@ def tile_locallyconnectednet_pa_kernel(
                         stop=(k == KK - 1),
                     )
                 nc.scalar.activation(
-                    out=biased_all[:, 2 * (i // 2) + j // 2, 2 * (i % 2) + j % 2, :],
+                    out=biased_all[:, 2 * (i % 2) + j % 2, :, 2 * (i // 2) + j // 2],
                     in_=acc[:],
                     func=RELU,
                     bias=b2_f32[:, i * OH + j : i * OH + j + 1],
                     scale=1.0,
                 )
 
-        def pool_windows(u):
-            for v in range(OH // 2):
-                with nc.allow_low_precision(reason="a maximum is exact; this is g's one rounding"):
-                    nc.vector.tensor_reduce(
-                        out=g_grouped[:, :, 2 * u + v],
-                        in_=biased_all[:, 2 * u + v].rearrange("p q n -> p n q"),
-                        axis=mybir.AxisListType.X,
-                        op=mybir.AluOpType.max,
-                    )
+        def maximum(out, in0, in1):
+            with nc.allow_low_precision(reason="a maximum is exact"):
+                nc.vector.tensor_tensor(out=out, in0=in0, in1=in1, op=mybir.AluOpType.max)
 
         for i in range(OH):
             quantise_w2_row(1, i)
@@ -280,8 +285,10 @@ def tile_locallyconnectednet_pa_kernel(
             if i == 0:
                 for s in late:
                     regroup(s, OH - 1, True)
-        pool_windows(0)
-        pool_windows(1)
+        positions = [biased_all[:, q].rearrange("p n w -> p (n w)") for q in range(4)]
+        maximum(tops[:, 0], positions[0], positions[1])
+        maximum(tops[:, 1], tops[:, 0], positions[2])
+        maximum(g_grouped.rearrange("p n t -> p (n t)"), tops[:, 1], positions[3])
 
         nc.vector.quantize_mx(
             out=g_codes.bitcast(FP8X4),
@@ -289,18 +296,26 @@ def tile_locallyconnectednet_pa_kernel(
             in_=g_grouped.rearrange("p n t -> p (n t)"),
         )
         fc_psum = dense_pool.tile([P, F], F32)
-        nc.tensor.matmul_mx(
-            out=fc_psum[:],
-            lhsT=g_codes.bitcast(FP8X4),
-            lhsT_scale=g_scales,
-            rhs=fc_codes.bitcast(FP8X4),
-            rhs_scale=fc_scales[:],
-            start=True,
-            stop=True,
-        )
         result = raw_pool.tile([P, F], F32, align_bytes=64, tag="raw")
-        nc.vector.tensor_tensor(
-            out=result[:], in0=fc_psum[:], in1=fc_b_all, op=mybir.AluOpType.add
+        for cols in (slice(0, F // 2), slice(F // 2, F)):
+            nc.tensor.matmul_mx(
+                out=fc_psum[:, cols],
+                lhsT=g_codes.bitcast(FP8X4),
+                lhsT_scale=g_scales,
+                rhs=fc_codes[:, cols].bitcast(FP8X4),
+                rhs_scale=fc_scales[:, cols],
+                start=True,
+                stop=True,
+            )
+        for cols in (slice(0, F // 2), slice(F // 2, F)):
+            nc.vector.tensor_tensor(
+                out=result[:, cols], in0=fc_psum[:, cols], in1=fc_b_all[:, cols], op=mybir.AluOpType.add
+            )
+        nc.scalar.activation(
+            out=result[:, : F // 2], in_=result[:, : F // 2], func=RELU, bias=0.0, scale=1.0
         )
-        nc.vector.tensor_scalar_max(out=result[:], in0=result[:], scalar1=0.0)
-        nc.sync.dma_start(out=out[:, :], in_=result[:])
+        nc.vector.tensor_scalar_max(
+            out=result[:, F // 2 :], in0=result[:, F // 2 :], scalar1=0.0
+        )
+        for cols in (slice(0, F // 2), slice(F // 2, F)):
+            nc.sync.dma_start(out=out[:, cols], in_=result[:, cols])

@@ -34,6 +34,8 @@ BANKS = 7
 RAW_BUFS = 5
 FLEX_LOAD = 13
 
+ALIGN = 256
+
 FLOPS = 2 * N * O * 512 * R + 2 * N * 512 * F
 
 
@@ -49,11 +51,11 @@ def tile_locallyconnectednet_pa_kernel(
             nc.vector.tensor_copy(out=out_view, in_=in_view)
 
     with (
-        tc.tile_pool(name="keep", bufs=1) as keep,
-        tc.tile_pool(name="big", bufs=1) as big,
         tc.tile_pool(name="raw", bufs=RAW_BUFS) as raw_pool,
         tc.tile_pool(name="flex", bufs=1) as flex,
+        tc.tile_pool(name="big", bufs=1) as big,
         tc.tile_pool(name="grouped", bufs=OH) as grouped_pool,
+        tc.tile_pool(name="keep", bufs=1) as keep,
         tc.psum_pool(name="bank", bufs=BANKS) as bank_pool,
         tc.psum_pool(name="dense", bufs=1) as dense_pool,
         tc.manual_schedule(),
@@ -65,8 +67,6 @@ def tile_locallyconnectednet_pa_kernel(
         b2_f32 = keep.tile([P, OH * OH], F32)
         ident = keep.tile([P, P], F32)
         make_identity(nc, ident[:])
-        fc_scales = keep.tile([P, F], U8, align_bytes=64)
-        nc.vector.memset(fc_scales[:].bitcast(I32), 0)
 
         nc.sync.dma_start(out=b2_bf[:], in_=b2.rearrange("o i j -> o (i j)"))
         h_raw = big.tile([P, C * PIXELS], BF16, align_bytes=64, tag="big")
@@ -83,9 +83,9 @@ def tile_locallyconnectednet_pa_kernel(
 
         def load_w2(s):
             if s == FLEX_LOAD:
-                raw = flex.tile([P, O_LOAD * PACK, R], BF16, align_bytes=64, tag="flex")
+                raw = flex.tile([P, O_LOAD * PACK, R], BF16, align_bytes=ALIGN, tag="flex")
             else:
-                raw = raw_pool.tile([P, O_LOAD * PACK, R], BF16, align_bytes=64, tag="raw")
+                raw = raw_pool.tile([P, O_LOAD * PACK, R], BF16, align_bytes=ALIGN, tag="raw")
             parts = 2 if s == LOADS - 1 else 1
             o_part = O_LOAD // parts
             for part in range(parts):
@@ -132,7 +132,7 @@ def tile_locallyconnectednet_pa_kernel(
             return 2
 
         words = h_raw[:].bitcast(F32).rearrange("n (p t s) -> n t s p", t=PACK, s=PAIRS)
-        h_grouped = flex.tile([P, H_SLOTS, PIXELS_QUANT, N * PACK], BF16, align_bytes=64, tag="flex")
+        h_grouped = flex.tile([P, H_SLOTS, PIXELS_QUANT, N * PACK], BF16, align_bytes=ALIGN, tag="flex")
         banks = {}
 
         def transpose_pair(s):
@@ -219,10 +219,12 @@ def tile_locallyconnectednet_pa_kernel(
         for i in range(OH):
             regroup(first_b + 2, i, i >= vector_rows(first_b + 2))
 
-        tail_words = raw_pool.tile([P, O_LOAD * PACK * R // 2], U32, align_bytes=64, tag="raw")
+        tail_words = raw_pool.tile([P, O_LOAD * PACK * R // 2], U32, align_bytes=ALIGN, tag="raw")
         fc_codes = tail_words[:, 0:F]
         g_codes = tail_words[:, F : F + N]
         g_scales = tail_words[:, 640:672].bitcast(U8)
+        fc_scales = tail_words[:, 704:832].bitcast(U8)
+        nc.gpsimd.memset(tail_words[:, 704:832], 0)
         nc.sync.dma_start(
             out=fc_codes.bitcast(I32),
             in_=fc1_w_words.rearrange("g p n t -> (g p) (n t)").bitcast(I32),
@@ -234,7 +236,7 @@ def tile_locallyconnectednet_pa_kernel(
             )
         for i in range(OH):
             regroup(first_b + 3, i, i >= vector_rows(first_b + 3))
-        tail_values = raw_pool.tile([P, 2, F], BF16, align_bytes=64, tag="raw")
+        tail_values = raw_pool.tile([P, 2, F], BF16, align_bytes=ALIGN, tag="raw")
         fc_b_all = tail_values[:, 0, :]
         g_grouped = tail_values[:, 1, :].rearrange("p (n t) -> p n t", t=PACK)
         nc.sync.dma_start(out=fc_b_all, in_=fc1_b.partition_broadcast(P))
@@ -249,8 +251,8 @@ def tile_locallyconnectednet_pa_kernel(
                 else:
                     regroup(s, i, i >= vector_rows(s))
 
-        biased_all = flex.tile([P, 4, N, PACK], BF16, align_bytes=64, tag="flex")
-        tops = raw_pool.tile([P, 2, N * PACK], BF16, align_bytes=64, tag="raw")
+        biased_all = flex.tile([P, 4, PACK, N], BF16, align_bytes=ALIGN, tag="flex")
+        tops = raw_pool.tile([P, 2, PACK, N], BF16, align_bytes=ALIGN, tag="raw")
 
         def convolve_row(i):
             for j in range(OH):
@@ -268,7 +270,7 @@ def tile_locallyconnectednet_pa_kernel(
                         stop=(k == KK - 1),
                     )
                 nc.scalar.activation(
-                    out=biased_all[:, 2 * (i % 2) + j % 2, :, 2 * (i // 2) + j // 2],
+                    out=biased_all[:, 2 * (i % 2) + j % 2, 2 * (i // 2) + j // 2, :],
                     in_=acc[:],
                     func=RELU,
                     bias=b2_f32[:, i * OH + j : i * OH + j + 1],
@@ -285,10 +287,13 @@ def tile_locallyconnectednet_pa_kernel(
             if i == 0:
                 for s in late:
                     regroup(s, OH - 1, True)
-        positions = [biased_all[:, q].rearrange("p n w -> p (n w)") for q in range(4)]
-        maximum(tops[:, 0], positions[0], positions[1])
-        maximum(tops[:, 1], tops[:, 0], positions[2])
-        maximum(g_grouped.rearrange("p n t -> p (n t)"), tops[:, 1], positions[3])
+        maximum(tops[:, 0], biased_all[:, 0], biased_all[:, 1])
+        maximum(tops[:, 1], tops[:, 0], biased_all[:, 2])
+        maximum(
+            g_grouped,
+            tops[:, 1].rearrange("p w n -> p n w"),
+            biased_all[:, 3].rearrange("p w n -> p n w"),
+        )
 
         nc.vector.quantize_mx(
             out=g_codes.bitcast(FP8X4),
@@ -296,7 +301,7 @@ def tile_locallyconnectednet_pa_kernel(
             in_=g_grouped.rearrange("p n t -> p (n t)"),
         )
         fc_psum = dense_pool.tile([P, F], F32)
-        result = raw_pool.tile([P, F], F32, align_bytes=64, tag="raw")
+        result = raw_pool.tile([P, F], F32, align_bytes=ALIGN, tag="raw")
         for cols in (slice(0, F // 2), slice(F // 2, F)):
             nc.tensor.matmul_mx(
                 out=fc_psum[:, cols],

@@ -54,7 +54,7 @@ def tile_locallyconnectednet_pa_kernel(
         tc.tile_pool(name="raw", bufs=RAW_BUFS) as raw_pool,
         tc.tile_pool(name="flex", bufs=1) as flex,
         tc.tile_pool(name="big", bufs=1) as big,
-        tc.tile_pool(name="grouped", bufs=OH) as grouped_pool,
+        tc.tile_pool(name="grouped", bufs=1) as grouped_pool,
         tc.tile_pool(name="keep", bufs=1) as keep,
         tc.psum_pool(name="bank", bufs=BANKS) as bank_pool,
         tc.psum_pool(name="dense", bufs=1) as dense_pool,
@@ -99,26 +99,35 @@ def tile_locallyconnectednet_pa_kernel(
                 )
             raws[s] = raw
 
-        def new_row(i):
-            row = grouped_pool.tile(
-                [P, KK, OH, O_HALF * PACK], BF16, align_bytes=64, name="w_row%d" % i, tag="grouped"
-            )
-            return row
-
-        rows = [[new_row(i) for i in range(OH)], [None] * OH]
+        grouped = grouped_pool.tile([P, OH, KK, OH, O_HALF * PACK], BF16, align_bytes=64)
 
         def regroup(s, i, on_scalar, first=0, count=O_LOAD * PACK):
-            half, load = divmod(s, LOADS_HALF)
-            a_first = load * O_LOAD * PACK + first
+            a_first = s % LOADS_HALF * O_LOAD * PACK + first
             copy(
                 on_scalar,
-                rows[half][i][:, :, :, a_first : a_first + count].rearrange(
+                grouped[:, i, :, :, a_first : a_first + count].rearrange(
                     "p k j (h a) -> p h k a j", h=2
                 ),
                 raws[s][:, first : first + count, :].rearrange(
                     "p (h a) (k i j) -> p i h k a j", h=2, k=KK, i=OH
                 )[:, i],
             )
+
+        def regroup_rows(s, rows, on_scalar):
+            rows = list(rows)
+            a_first = s % LOADS_HALF * O_LOAD * PACK
+            while len(rows) > 1:
+                i = rows[0]
+                copy(
+                    on_scalar,
+                    grouped[:, i : i + 2, :, :, a_first : a_first + O_LOAD * PACK].rearrange(
+                        "p i k j a -> p i k a j"
+                    ),
+                    raws[s][:].rearrange("p a (k i j) -> p i k a j", k=KK, i=OH)[:, i : i + 2],
+                )
+                rows = rows[2:]
+            for i in rows:
+                regroup(s, i, on_scalar)
 
         for s in range(RAW_BUFS):
             load_w2(s)
@@ -174,14 +183,19 @@ def tile_locallyconnectednet_pa_kernel(
                 if BANKS + s < PAIRS:
                     transpose_pair(BANKS + s)
             load, i = divmod(s - 4, OH)
-            regroup(load, i, False)
+            if i % 2 == 0:
+                regroup_rows(load, (i, i + 1), False)
             if s < PAIRS:
                 quantise_h(s)
             if i == OH - 1:
                 load_w2(load + RAW_BUFS)
         for s in range(4, LOADS_HALF):
-            for i in range(OH):
-                regroup(s, i, i >= vector_rows(s))
+            regroup_rows(s, range(vector_rows(s)), False)
+            if s == LOADS_HALF - 1:
+                for i in range(1, OH):
+                    regroup(s, i, True)
+            else:
+                regroup_rows(s, range(vector_rows(s), OH), True)
             load_w2(s + RAW_BUFS)
         load_w2(FLEX_LOAD)
 
@@ -194,30 +208,26 @@ def tile_locallyconnectednet_pa_kernel(
                     nc.vector.quantize_mx(
                         out=w_codes[:, first : first + O_HALF].bitcast(FP8X4),
                         scales=w_scales[:, first : first + O_HALF],
-                        in_=rows[half][i][:, k, j, :],
+                        in_=grouped[:, i, k, j, :],
                     )
 
         first_b = LOADS_HALF
         quantise_w2_row(0, 0)
-        rows[1][0] = new_row(0)
         regroup(first_b, 0, True)
         quantise_w2_row(0, 1)
-        rows[1][1] = new_row(1)
         regroup(first_b, 1, True)
         regroup(first_b + 1, 0, True)
         quantise_w2_row(0, 2)
-        rows[1][2] = new_row(2)
         regroup(first_b, 2, True)
         regroup(first_b + 1, 1, True)
         regroup(first_b + 1, 2, True)
         quantise_w2_row(0, 3)
-        rows[1][3] = new_row(3)
         regroup(first_b, 3, False)
         load_w2(14)
         regroup(first_b + 1, 3, False)
         load_w2(15)
-        for i in range(OH):
-            regroup(first_b + 2, i, i >= vector_rows(first_b + 2))
+        for on_scalar, rows in ((False, range(2)), (True, range(2, OH))):
+            regroup_rows(first_b + 2, rows, on_scalar)
 
         tail_words = raw_pool.tile([P, O_LOAD * PACK * R // 2], U32, align_bytes=ALIGN, tag="raw")
         fc_codes = tail_words[:, 0:F]
@@ -234,25 +244,25 @@ def tile_locallyconnectednet_pa_kernel(
                 out=fc_scales[32 * quadrant : 32 * quadrant + 4, :].bitcast(I32),
                 in_=fc1_w_scales[0, 4 * quadrant : 4 * quadrant + 4, :].bitcast(I32),
             )
-        for i in range(OH):
-            regroup(first_b + 3, i, i >= vector_rows(first_b + 3))
+        for on_scalar, rows in ((False, range(2)), (True, range(2, OH))):
+            regroup_rows(first_b + 3, rows, on_scalar)
         tail_values = raw_pool.tile([P, 2, F], BF16, align_bytes=ALIGN, tag="raw")
         fc_b_all = tail_values[:, 0, :]
         g_grouped = tail_values[:, 1, :].rearrange("p (n t) -> p n t", t=PACK)
         nc.sync.dma_start(out=fc_b_all, in_=fc1_b.partition_broadcast(P))
-        late = []
+        late = range(LOADS - 3, LOADS)
         for s in range(first_b + 4, LOADS):
-            for i in range(OH):
-                if i == OH - 1 and s >= LOADS - 2:
-                    late.append(s)
-                elif i == 0 and s == LOADS - 1:
-                    for part in range(2):
-                        regroup(s, i, False, part * O_LOAD * PACK // 2, O_LOAD * PACK // 2)
-                else:
-                    regroup(s, i, i >= vector_rows(s))
+            if s == LOADS - 1:
+                for part in range(2):
+                    regroup(s, 0, False, part * O_LOAD * PACK // 2, O_LOAD * PACK // 2)
+                for i in (1, 2):
+                    regroup(s, i, True)
+            else:
+                regroup_rows(s, range(vector_rows(s)), False)
+                regroup_rows(s, range(vector_rows(s), OH - 1 if s in late else OH), True)
 
-        biased_all = flex.tile([P, 4, PACK, N], BF16, align_bytes=ALIGN, tag="flex")
-        tops = raw_pool.tile([P, 2, PACK, N], BF16, align_bytes=ALIGN, tag="raw")
+        biased_all = raw_pool.tile([P, 4, PACK, N], BF16, align_bytes=ALIGN, tag="raw")
+        tops = flex.tile([P, 2, PACK, N], BF16, align_bytes=ALIGN, tag="flex")
 
         def convolve_row(i):
             for j in range(OH):

@@ -36,6 +36,8 @@ FLEX_LOAD = 13
 
 ALIGN = 256
 
+TURNED = (10, 11, 12)
+
 FLOPS = 2 * N * O * 512 * R + 2 * N * 512 * F
 
 
@@ -67,6 +69,7 @@ def tile_locallyconnectednet_pa_kernel(
         b2_f32 = keep.tile([P, OH * OH], F32)
         ident = keep.tile([P, P], F32)
         make_identity(nc, ident[:])
+        ident_bf = ident[:].bitcast(BF16)[:, 1::2]
 
         nc.sync.dma_start(out=b2_bf[:], in_=b2.rearrange("o i j -> o (i j)"))
         h_raw = big.tile([P, C * PIXELS], BF16, align_bytes=64, tag="big")
@@ -113,8 +116,30 @@ def tile_locallyconnectednet_pa_kernel(
                 )[:, i],
             )
 
+        def turn(s, i):
+            a_first = s % LOADS_HALF * O_LOAD * PACK
+            source = raws[s][:].rearrange("p a (k i j) -> p i a k j", k=KK, i=OH)[:, i]
+            for first, count in ((0, 2 * KS), (2 * KS, KS)):
+                bank = bank_pool.tile([P, count, OH, O_LOAD * PACK], BF16, tag="bank")
+                for k in range(0, count, KS):
+                    nc.tensor.matmul(
+                        bank[:, k : k + KS].rearrange("p k j a -> p a k j"),
+                        lhsT=ident_bf,
+                        rhs=source[:, :, first + k : first + k + KS],
+                        start=True,
+                        stop=True,
+                    )
+                nc.scalar.copy(
+                    out=grouped[:, i, first : first + count, :, a_first : a_first + O_LOAD * PACK],
+                    in_=bank[:],
+                )
+
         def regroup_rows(s, rows, on_scalar):
             rows = list(rows)
+            if on_scalar and s in TURNED:
+                for i in rows:
+                    turn(s, i)
+                return
             a_first = s % LOADS_HALF * O_LOAD * PACK
             while len(rows) > 1:
                 i = rows[0]
@@ -136,8 +161,6 @@ def tile_locallyconnectednet_pa_kernel(
             left = LOADS_HALF - 1 - s % LOADS_HALF
             if left == 0:
                 return 1
-            if s == LOADS - 3:
-                return 3
             return 2
 
         words = h_raw[:].bitcast(F32).rearrange("n (p t s) -> n t s p", t=PACK, s=PAIRS)
@@ -226,8 +249,8 @@ def tile_locallyconnectednet_pa_kernel(
         load_w2(14)
         regroup(first_b + 1, 3, False)
         load_w2(15)
-        for on_scalar, rows in ((False, range(2)), (True, range(2, OH))):
-            regroup_rows(first_b + 2, rows, on_scalar)
+        regroup_rows(first_b + 2, range(vector_rows(first_b + 2)), False)
+        regroup_rows(first_b + 2, range(vector_rows(first_b + 2), OH), True)
 
         tail_words = raw_pool.tile([P, O_LOAD * PACK * R // 2], U32, align_bytes=ALIGN, tag="raw")
         fc_codes = tail_words[:, 0:F]
@@ -244,8 +267,8 @@ def tile_locallyconnectednet_pa_kernel(
                 out=fc_scales[32 * quadrant : 32 * quadrant + 4, :].bitcast(I32),
                 in_=fc1_w_scales[0, 4 * quadrant : 4 * quadrant + 4, :].bitcast(I32),
             )
-        for on_scalar, rows in ((False, range(2)), (True, range(2, OH))):
-            regroup_rows(first_b + 3, rows, on_scalar)
+        regroup_rows(first_b + 3, range(vector_rows(first_b + 3)), False)
+        regroup_rows(first_b + 3, range(vector_rows(first_b + 3), OH), True)
         tail_values = raw_pool.tile([P, 2, F], BF16, align_bytes=ALIGN, tag="raw")
         fc_b_all = tail_values[:, 0, :]
         g_grouped = tail_values[:, 1, :].rearrange("p (n t) -> p n t", t=PACK)

import concourse.mybir as mybir
from concourse.masks import make_identity

F32 = mybir.dt.float32
BF16 = mybir.dt.bfloat16
I32 = mybir.dt.int32
U32 = mybir.dt.uint32
U8 = mybir.dt.uint8
FP8X4 = mybir.dt.float8_e4m3fn_x4
RELU = mybir.ActivationFunctionType.Relu

P = 128
PACK = 4
N = 128
O = 128
C = 512
KS = 3
KK = KS * KS
H = 6
PIXELS = H * H
PAIRS = PIXELS // 2
OH = 4
R = KK * OH * OH
F = 512

O_HALF = O // 2
O_LOAD = 8
LOADS = O // O_LOAD
LOADS_HALF = O_HALF // O_LOAD
H_LOADS = 4
PIXELS_QUANT = 2
H_SLOTS = 4
BANKS = 7
RAW_BUFS = 5
FLEX_LOAD = 13

ALIGN = 256

TURNED = (10, 11, 12)

FLOPS = 2 * N * O * 512 * R + 2 * N * 512 * F


def tile_locallyconnectednet_pa_kernel(
    tc, h_pool1, w2, b2, fc1_w_words, fc1_w_scales, fc1_b, out
):
    nc = tc.nc

    def copy(on_scalar, out_view, in_view):
        if on_scalar:
            nc.scalar.copy(out=out_view, in_=in_view)
        else:
            nc.vector.tensor_copy(out=out_view, in_=in_view)

    with (
        tc.tile_pool(name="raw", bufs=RAW_BUFS) as raw_pool,
        tc.tile_pool(name="flex", bufs=1) as flex,
        tc.tile_pool(name="big", bufs=1) as big,
        tc.tile_pool(name="grouped", bufs=1) as grouped_pool,
        tc.tile_pool(name="keep", bufs=1) as keep,
        tc.psum_pool(name="bank", bufs=BANKS) as bank_pool,
        tc.psum_pool(name="dense", bufs=1) as dense_pool,
        tc.manual_schedule(),
    ):
        w_scales = keep.tile([P, R * O], U8, align_bytes=64)
        h_codes = keep.tile([P, PIXELS * N], U32, align_bytes=64)
        h_scales = keep.tile([P, PIXELS * N], U8, align_bytes=64)
        b2_bf = keep.tile([P, OH * OH], BF16)
        b2_f32 = keep.tile([P, OH * OH], F32)
        ident = keep.tile([P, P], F32)
        make_identity(nc, ident[:])
        ident_bf = ident[:].bitcast(BF16)[:, 1::2]

        nc.sync.dma_start(out=b2_bf[:], in_=b2.rearrange("o i j -> o (i j)"))
        h_raw = big.tile([P, C * PIXELS], BF16, align_bytes=64, tag="big")
        h_flat = h_pool1.rearrange("n c y x -> n (c y x)")
        h_step = C * PIXELS // H_LOADS
        for load in range(H_LOADS):
            nc.sync.dma_start(
                out=h_raw[:, load * h_step : (load + 1) * h_step],
                in_=h_flat[:, load * h_step : (load + 1) * h_step],
            )
        nc.vector.tensor_copy(out=b2_f32[:], in_=b2_bf[:])

        raws = {}

        def load_w2(s):
            if s == FLEX_LOAD:
                raw = flex.tile([P, O_LOAD * PACK, R], BF16, align_bytes=ALIGN, tag="flex")
            else:
                raw = raw_pool.tile([P, O_LOAD * PACK, R], BF16, align_bytes=ALIGN, tag="raw")
            parts = 2 if s == LOADS - 1 else 1
            o_part = O_LOAD // parts
            for part in range(parts):
                nc.sync.dma_start(
                    out=raw[:, part * o_part * PACK : (part + 1) * o_part * PACK, :].rearrange(
                        "p (o t) r -> p o (t r)", t=PACK
                    ),
                    in_=w2[s * O_LOAD + part * o_part : s * O_LOAD + (part + 1) * o_part].rearrange(
                        "o (p t) k i j -> p o (t k i j)", t=PACK
                    ),
                )
            raws[s] = raw

        grouped = grouped_pool.tile([P, OH, KK, OH, O_HALF * PACK], BF16, align_bytes=64)

        def regroup(s, i, on_scalar, first=0, count=O_LOAD * PACK):
            a_first = s % LOADS_HALF * O_LOAD * PACK + first
            copy(
                on_scalar,
                grouped[:, i, :, :, a_first : a_first + count].rearrange(
                    "p k j (h a) -> p h k a j", h=2
                ),
                raws[s][:, first : first + count, :].rearrange(
                    "p (h a) (k i j) -> p i h k a j", h=2, k=KK, i=OH
                )[:, i],
            )

        def turn(s, i):
            a_first = s % LOADS_HALF * O_LOAD * PACK
            source = raws[s][:].rearrange("p a (k i j) -> p i a k j", k=KK, i=OH)[:, i]
            for first, count in ((0, 2 * KS), (2 * KS, KS)):
                bank = bank_pool.tile([P, count, OH, O_LOAD * PACK], BF16, tag="bank")
                for k in range(0, count, KS):
                    nc.tensor.matmul(
                        bank[:, k : k + KS].rearrange("p k j a -> p a k j"),
                        lhsT=ident_bf,
                        rhs=source[:, :, first + k : first + k + KS],
                        start=True,
                        stop=True,
                    )
                nc.scalar.copy(
                    out=grouped[:, i, first : first + count, :, a_first : a_first + O_LOAD * PACK],
                    in_=bank[:],
                )

        def regroup_rows(s, rows, on_scalar):
            rows = list(rows)
            if on_scalar and s in TURNED:
                for i in rows:
                    turn(s, i)
                return
            a_first = s % LOADS_HALF * O_LOAD * PACK
            while len(rows) > 1:
                i = rows[0]
                copy(
                    on_scalar,
                    grouped[:, i : i + 2, :, :, a_first : a_first + O_LOAD * PACK].rearrange(
                        "p i k j a -> p i k a j"
                    ),
                    raws[s][:].rearrange("p a (k i j) -> p i k a j", k=KK, i=OH)[:, i : i + 2],
                )
                rows = rows[2:]
            for i in rows:
                regroup(s, i, on_scalar)

        for s in range(RAW_BUFS):
            load_w2(s)

        def vector_rows(s):
            left = LOADS_HALF - 1 - s % LOADS_HALF
            if left == 0:
                return 1
            return 2

        words = h_raw[:].bitcast(F32).rearrange("n (p t s) -> n t s p", t=PACK, s=PAIRS)
        h_grouped = flex.tile([P, H_SLOTS, PIXELS_QUANT, N * PACK], BF16, align_bytes=ALIGN, tag="flex")
        banks = {}

        def transpose_pair(s):
            xt = bank_pool.tile([P, PACK, N], F32, tag="bank")
            for t in range(PACK):
                nc.tensor.transpose(xt[:, t, :], words[:, t, s, :], ident[:])
            banks[s] = xt

        def copy_out(s, on_scalar):
            copy(
                on_scalar,
                h_grouped[:, s % H_SLOTS].rearrange("p e (n t) -> p e n t", t=PACK),
                banks[s][:]
                .rearrange("p t n -> p (t n)")
                .bitcast(BF16)
                .rearrange("p (t n e) -> p e n t", t=PACK, e=2),
            )

        def quantise_h(m):
            first = m * PIXELS_QUANT * N
            nc.vector.quantize_mx(
                out=h_codes[:, first : first + PIXELS_QUANT * N].bitcast(FP8X4),
                scales=h_scales[:, first : first + PIXELS_QUANT * N],
                in_=h_grouped[:, m % H_SLOTS].rearrange("p x a -> p (x a)"),
            )

        for s in range(BANKS):
            transpose_pair(s)
        for s in range(4):
            copy_out(s, s % 2 == 0)
            transpose_pair(BANKS + s)
            if s % 2 == 1:
                quantise_h(s - 1)
                quantise_h(s)

        for s in range(4, PAIRS + 2):
            if s < PAIRS:
                copy_out(s, True)
                if BANKS + s < PAIRS:
                    transpose_pair(BANKS + s)
            load, i = divmod(s - 4, OH)
            if i % 2 == 0:
                regroup_rows(load, (i, i + 1), False)
            if s < PAIRS:
                quantise_h(s)
            if i == OH - 1:
                load_w2(load + RAW_BUFS)
        for s in range(4, LOADS_HALF):
            regroup_rows(s, range(vector_rows(s)), False)
            if s == LOADS_HALF - 1:
                for i in range(1, OH):
                    regroup(s, i, True)
            else:
                regroup_rows(s, range(vector_rows(s), OH), True)
            load_w2(s + RAW_BUFS)
        load_w2(FLEX_LOAD)

        w_codes = big.tile([P, R * O], U32, align_bytes=64, tag="big")

        def quantise_w2_row(half, i):
            for j in range(OH):
                for k in range(KK):
                    first = ((k * OH + i) * OH + j) * O + half * O_HALF
                    nc.vector.quantize_mx(
                        out=w_codes[:, first : first + O_HALF].bitcast(FP8X4),
                        scales=w_scales[:, first : first + O_HALF],
                        in_=grouped[:, i, k, j, :],
                    )

        first_b = LOADS_HALF
        quantise_w2_row(0, 0)
        regroup(first_b, 0, True)
        quantise_w2_row(0, 1)
        regroup(first_b, 1, True)
        regroup(first_b + 1, 0, True)
        quantise_w2_row(0, 2)
        regroup(first_b, 2, True)
        regroup(first_b + 1, 1, True)
        regroup(first_b + 1, 2, True)
        quantise_w2_row(0, 3)
        regroup(first_b, 3, False)
        load_w2(14)
        regroup(first_b + 1, 3, False)
        load_w2(15)
        regroup_rows(first_b + 2, range(vector_rows(first_b + 2)), False)
        regroup_rows(first_b + 2, range(vector_rows(first_b + 2), OH), True)

        tail_words = raw_pool.tile([P, O_LOAD * PACK * R // 2], U32, align_bytes=ALIGN, tag="raw")
        fc_codes = tail_words[:, 0:F]
        g_codes = tail_words[:, F : F + N]
        g_scales = tail_words[:, 640:672].bitcast(U8)
        fc_scales = tail_words[:, 704:832].bitcast(U8)
        nc.gpsimd.memset(tail_words[:, 704:832], 0)
        nc.sync.dma_start(
            out=fc_codes.bitcast(I32),
            in_=fc1_w_words.rearrange("g p n t -> (g p) (n t)").bitcast(I32),
        )
        for quadrant in range(4):
            nc.sync.dma_start(
                out=fc_scales[32 * quadrant : 32 * quadrant + 4, :].bitcast(I32),
                in_=fc1_w_scales[0, 4 * quadrant : 4 * quadrant + 4, :].bitcast(I32),
            )
        regroup_rows(first_b + 3, range(vector_rows(first_b + 3)), False)
        regroup_rows(first_b + 3, range(vector_rows(first_b + 3), OH), True)
        tail_values = raw_pool.tile([P, 2, F], BF16, align_bytes=ALIGN, tag="raw")
        fc_b_all = tail_values[:, 0, :]
        g_grouped = tail_values[:, 1, :].rearrange("p (n t) -> p n t", t=PACK)
        nc.sync.dma_start(out=fc_b_all, in_=fc1_b.partition_broadcast(P))
        late = range(LOADS - 3, LOADS)
        for s in range(first_b + 4, LOADS):
            if s == LOADS - 1:
                for part in range(2):
                    regroup(s, 0, False, part * O_LOAD * PACK // 2, O_LOAD * PACK // 2)
                for i in (1, 2):
                    regroup(s, i, True)
            else:
                regroup_rows(s, range(vector_rows(s)), False)
                regroup_rows(s, range(vector_rows(s), OH - 1 if s in late else OH), True)

        biased_all = raw_pool.tile([P, 4, PACK, N], BF16, align_bytes=ALIGN, tag="raw")
        tops = flex.tile([P, 2, PACK, N], BF16, align_bytes=ALIGN, tag="flex")

        def convolve_row(i):
            for j in range(OH):
                acc = bank_pool.tile([P, N], F32, tag="bank")
                for k in range(KK):
                    r = (k * OH + i) * OH + j
                    x = (i + k // KS) * H + j + k % KS
                    nc.tensor.matmul_mx(
                        out=acc[:],
                        lhsT=w_codes[:, r * O : (r + 1) * O].bitcast(FP8X4),
                        lhsT_scale=w_scales[:, r * O : (r + 1) * O],
                        rhs=h_codes[:, x * N : (x + 1) * N].bitcast(FP8X4),
                        rhs_scale=h_scales[:, x * N : (x + 1) * N],
                        start=(k == 0),
                        stop=(k == KK - 1),
                    )
                nc.scalar.activation(
                    out=biased_all[:, 2 * (i % 2) + j % 2, 2 * (i // 2) + j // 2, :],
                    in_=acc[:],
                    func=RELU,
                    bias=b2_f32[:, i * OH + j : i * OH + j + 1],
                    scale=1.0,
                )

        def maximum(out, in0, in1):
            with nc.allow_low_precision(reason="a maximum is exact"):
                nc.vector.tensor_tensor(out=out, in0=in0, in1=in1, op=mybir.AluOpType.max)

        for i in range(OH):
            quantise_w2_row(1, i)
            convolve_row(i)
            if i == 0:
                for s in late:
                    regroup(s, OH - 1, True)
        maximum(tops[:, 0], biased_all[:, 0], biased_all[:, 1])
        maximum(tops[:, 1], tops[:, 0], biased_all[:, 2])
        maximum(
            g_grouped,
            tops[:, 1].rearrange("p w n -> p n w"),
            biased_all[:, 3].rearrange("p w n -> p n w"),
        )

        nc.vector.quantize_mx(
            out=g_codes.bitcast(FP8X4),
            scales=g_scales,
            in_=g_grouped.rearrange("p n t -> p (n t)"),
        )
        fc_psum = dense_pool.tile([P, F], F32)
        result = raw_pool.tile([P, F], F32, align_bytes=ALIGN, tag="raw")
        for cols in (slice(0, F // 2), slice(F // 2, F)):
            nc.tensor.matmul_mx(
                out=fc_psum[:, cols],
                lhsT=g_codes.bitcast(FP8X4),
                lhsT_scale=g_scales,
                rhs=fc_codes[:, cols].bitcast(FP8X4),
                rhs_scale=fc_scales[:, cols],
                start=True,
                stop=True,
            )
        for cols in (slice(0, F // 2), slice(F // 2, F)):
            nc.vector.tensor_tensor(
                out=result[:, cols], in0=fc_psum[:, cols], in1=fc_b_all[:, cols], op=mybir.AluOpType.add
            )
        nc.scalar.activation(
            out=result[:, : F // 2], in_=result[:, : F // 2], func=RELU, bias=0.0, scale=1.0
        )
        nc.vector.tensor_scalar_max(
            out=result[:, F // 2 :], in0=result[:, F // 2 :], scalar1=0.0
        )
        for cols in (slice(0, F // 2), slice(F // 2, F)):
            nc.sync.dma_start(out=out[:, cols], in_=result[:, cols])
